import numpy as np
import ml_dtypes


def mxq(x, axis, fmt="e4m3"):
    dtype, down = {"e4m3": (ml_dtypes.float8_e4m3fn, 7), "e5m2": (ml_dtypes.float8_e5m2, 14)}[fmt]
    v = np.moveaxis(np.asarray(x, np.float32).astype(ml_dtypes.bfloat16).astype(np.float64), axis, -1)
    blocks = v.reshape(v.shape[:-1] + (-1, 32))
    amax = np.abs(blocks).max(-1, keepdims=True)
    byte = np.maximum(np.where(amax > 0, np.frexp(amax)[1] - 1 + 127, 0) - down, 1)
    scale = np.exp2(byte - 127.0)
    codes = (blocks / scale).astype(np.float32).astype(dtype).astype(np.float64)
    return np.moveaxis((codes * scale).reshape(v.shape), -1, axis)


WIDE = False


def mx_kscale(k):
    if not WIDE:
        return np.ones(k)
    levels = np.array([10, -10, 5, -5, 0])
    a = np.random.permutation(np.resize(levels, k // 512 * 4)).reshape(k // 512, 4)
    idx = np.arange(k)
    return np.exp2(a[idx // 512, idx % 128 // 32])


BF16 = ml_dtypes.bfloat16


def bf(x):
    return np.asarray(x, np.float32).astype(BF16)


def f64(x):
    return np.asarray(x).astype(np.float64)


B, S, D, NH = 2, 512, 1024, 8
SCALE = np.sqrt(D // NH)


def setup_inputs():
    s, t = mx_kscale(D), mx_kscale(D)
    return {"x": bf(np.random.standard_normal((B, S, D)) * s),
            "wq": bf(np.random.standard_normal((D, D)) * 0.84 / np.sqrt(D) / s[None, :] * t[:, None]),
            "wk": bf(np.random.standard_normal((D, D)) * 0.84 / np.sqrt(D) / s[None, :] / t[:, None])}


def reference(x, wq, wk):
    xq = mxq(f64(x), 2, "e4m3")
    q = xq @ mxq(f64(wq), 1, "e4m3").T
    k = xq @ mxq(f64(wk), 1, "e4m3").T
    sc = (mxq(q, 2, "e4m3") @ mxq(k, 2, "e4m3").transpose(0, 2, 1)) / SCALE
    e = np.exp(sc - sc.max(-1, keepdims=True))
    return e / e.sum(-1, keepdims=True)

@@ -1,0 +1,200 @@
+from contextlib import ExitStack
+import math
+
+import concourse.mybir as mybir
+from concourse.masks import make_identity
+
+F32 = mybir.dt.float32
+BF16 = mybir.dt.bfloat16
+U32 = mybir.dt.uint32
+U8 = mybir.dt.uint8
+FP8X4 = mybir.dt.float8_e4m3fn_x4
+EXP = mybir.ActivationFunctionType.Exp
+
+P = 128
+PACK = 4
+K_PASS = P * PACK
+B, S, D = 2, 512, 1024
+PASSES = D // K_PASS
+TILES = S // P
+WORDS = D // 2
+INV_SQRT = 1.0 / math.sqrt(D // 8)
+
+FLOPS = 2 * (2 * B * S * D * D) + 2 * B * S * S * D
+
+
+def tile_attentionnet_pa_kernel(tc, x, wq, wk, out):
+    nc = tc.nc
+    with ExitStack() as ctx:
+        keep = ctx.enter_context(tc.tile_pool(name="keep", bufs=1))
+        stage = ctx.enter_context(tc.tile_pool(name="stage", bufs=4))
+        small = ctx.enter_context(tc.tile_pool(name="small", bufs=4))
+        work = ctx.enter_context(tc.psum_pool(name="work", bufs=6))
+        score_pool = ctx.enter_context(tc.psum_pool(name="score_pool", bufs=2))
+
+        identity = keep.tile([P, P], F32, name="identity")
+        make_identity(nc, identity[:])
+        zero = keep.tile([P, 1], F32, name="zero")
+        one = keep.tile([P, 1], F32, name="one")
+        nc.vector.memset(zero[:], 0.0)
+        nc.scalar.activation(out=one[:], in_=zero[:], func=EXP)
+
+        def chunk_of_weights(w, g):
+            return w.rearrange("(g p j) k -> g p j k", p=P, j=PACK)[g]
+
+        def chunk_of_tokens(b):
+            return x[b].rearrange("(i p) k -> p i k", p=P)
+
+        sources = {
+            "k0": chunk_of_weights(wk, 0),
+            "x0": chunk_of_tokens(0),
+            "k1": chunk_of_weights(wk, 1),
+            "q0": chunk_of_weights(wq, 0),
+            "q1": chunk_of_weights(wq, 1),
+            "x1": chunk_of_tokens(1),
+        }
+        raw = {}
+        in_codes = {}
+        in_scales = {}
+        for name, source in sources.items():
+            raw[name] = keep.tile([P, TILES * D], BF16, name="raw_" + name)
+            in_codes[name] = keep.tile(
+                [P, TILES * PASSES * P], U32, name="codes_" + name, align_bytes=64
+            )
+            in_scales[name] = keep.tile(
+                [P, TILES * PASSES * P], U8, name="scales_" + name, align_bytes=64
+            )
+            rows = raw[name][:].rearrange("p (r k) -> p r k", r=TILES)
+            if name in ("k0", "x0"):
+                for r in range(TILES):
+                    nc.sync.dma_start(out=rows[:, r, :], in_=source[:, r, :])
+            else:
+                nc.sync.dma_start(out=rows, in_=source)
+
+        def block(tile, r, c):
+            first = (r * PASSES + c) * P
+            return tile[:, first : first + P]
+
+        def transpose_chunk(name):
+            words = raw[name][:].bitcast(F32)
+            for r in range(TILES):
+                bank = work.tile([P, PASSES, 2, P], F32, tag="work")
+                for c in range(PASSES):
+                    for u in range(2):
+                        first = r * WORDS + (2 * c + u) * P
+                        nc.tensor.transpose(
+                            bank[:, c, u, :], words[:, first : first + P], identity[:]
+                        )
+                grouped = stage.tile(
+                    [P, PASSES * P * PACK], BF16, tag="grouped_in", align_bytes=64
+                )
+                dst = grouped[:].bitcast(F32).rearrange(
+                    "p (c r u) -> p c r u", c=PASSES, u=2
+                )
+                src = bank[:].rearrange("p c u r -> p c r u")
+                if r % 2 == 0:
+                    nc.scalar.copy(out=dst, in_=src)
+                else:
+                    nc.vector.tensor_copy(out=dst, in_=src)
+                first = r * PASSES * P
+                nc.vector.quantize_mx(
+                    out=in_codes[name][:, first : first + PASSES * P].bitcast(FP8X4),
+                    scales=in_scales[name][:, first : first + PASSES * P],
+                    in_=grouped[:],
+                )
+
+        qk_codes = {}
+        qk_scales = {}
+        for name in ("q", "k"):
+            for b in range(B):
+                qk_codes[name, b] = keep.tile(
+                    [P, PASSES * S], U32, name="proj_codes_%s%d" % (name, b), align_bytes=64
+                )
+                qk_scales[name, b] = keep.tile(
+                    [P, PASSES * S], U8, name="proj_scales_%s%d" % (name, b), align_bytes=64
+                )
+
+        def project(name, g, b, i):
+            w = "%s%d" % (name, g)
+            xb = "x%d" % b
+            bank = work.tile([P, PACK, P], F32, tag="work")
+            for t in range(PACK):
+                for c in range(PASSES):
+                    nc.tensor.matmul_mx(
+                        out=bank[:, t, :],
+                        lhsT=block(in_codes[w], t, c).bitcast(FP8X4),
+                        lhsT_scale=block(in_scales[w], t, c),
+                        rhs=block(in_codes[xb], i, c).bitcast(FP8X4),
+                        rhs_scale=block(in_scales[xb], i, c),
+                        start=(c == 0),
+                        stop=(c == PASSES - 1),
+                    )
+            grouped = stage.tile([P, P * PACK], BF16, tag="grouped_qk", align_bytes=64)
+            nc.scalar.copy(
+                out=grouped[:].rearrange("p (r t) -> p r t", t=PACK),
+                in_=bank[:].rearrange("p t r -> p r t"),
+            )
+            first = g * S + i * P
+            nc.vector.quantize_mx(
+                out=qk_codes[name, b][:, first : first + P].bitcast(FP8X4),
+                scales=qk_scales[name, b][:, first : first + P],
+                in_=grouped[:],
+            )
+
+        def attend(b, i):
+            score = score_pool.tile([P, S], F32, tag="score")
+            for g in range(PASSES):
+                first = g * S + i * P
+                nc.tensor.matmul_mx(
+                    out=score[:],
+                    lhsT=qk_codes["q", b][:, first : first + P].bitcast(FP8X4),
+                    lhsT_scale=qk_scales["q", b][:, first : first + P],
+                    rhs=qk_codes["k", b][:, g * S : (g + 1) * S].bitcast(FP8X4),
+                    rhs_scale=qk_scales["k", b][:, g * S : (g + 1) * S],
+                    start=(g == 0),
+                    stop=(g == PASSES - 1),
+                )
+            row_max = small.tile([P, 1], F32, tag="row_max")
+            nc.vector.reduce_max(out=row_max[:], in_=score[:], axis=mybir.AxisListType.X)
+            shift = small.tile([P, 1], F32, tag="shift")
+            nc.vector.tensor_scalar_mul(out=shift[:], in0=row_max[:], scalar1=-INV_SQRT)
+            weights = stage.tile([P, S], F32, tag="weights")
+            row_sum = small.tile([P, 1], F32, tag="row_sum")
+            nc.scalar.activation(
+                out=weights[:],
+                in_=score[:],
+                func=EXP,
+                bias=shift[:],
+                scale=INV_SQRT,
+                accum_out=row_sum[:],
+            )
+            inverse = small.tile([P, 1], F32, tag="inverse")
+            nc.vector.reciprocal(out=inverse[:], in_=row_sum[:])
+            nc.vector.tensor_scalar_mul(out=weights[:], in0=weights[:], scalar1=inverse[:])
+            nc.sync.dma_start(out=out[b, i * P : (i + 1) * P, :], in_=weights[:])
+
+        def project_chunk(name, g, b):
+            for i in range(TILES):
+                project(name, g, b, i)
+
+        def project_and_attend(b):
+            for i in range(TILES):
+                project("q", 1, b, i)
+                if i > 0:
+                    attend(b, i - 1)
+            attend(b, TILES - 1)
+
+        transpose_chunk("k0")
+        transpose_chunk("x0")
+        project_chunk("k", 0, 0)
+        transpose_chunk("k1")
+        transpose_chunk("q0")
+        project_chunk("k", 1, 0)
+        transpose_chunk("q1")
+        project_chunk("q", 0, 0)
+        transpose_chunk("x1")
+        project_and_attend(0)
+        project_chunk("k", 0, 1)
+        project_chunk("k", 1, 1)
+        project_chunk("q", 0, 1)
+        project_and_attend(1)

@@ -31,6 +31,7 @@ def tile_attentionnet_pa_kernel(tc, x, wq, wk, out):
         small = ctx.enter_context(tc.tile_pool(name="small", bufs=4))
         work = ctx.enter_context(tc.psum_pool(name="work", bufs=6))
         score_pool = ctx.enter_context(tc.psum_pool(name="score_pool", bufs=2))
+        ctx.enter_context(tc.manual_schedule())
 
         identity = keep.tile([P, P], F32, name="identity")
         make_identity(nc, identity[:])
@@ -71,12 +72,28 @@ def tile_attentionnet_pa_kernel(tc, x, wq, wk, out):
             else:
                 nc.sync.dma_start(out=rows, in_=source)
 
-        def block(tile, r, c):
+        def block(codes_or_scales, r, c):
             first = (r * PASSES + c) * P
-            return tile[:, first : first + P]
+            return codes_or_scales[:, first : first + P]
+
+        def empty_bank(n, dst, src):
+            if n % 4 == 1:
+                nc.vector.tensor_copy(out=dst, in_=src)
+            else:
+                nc.scalar.copy(out=dst, in_=src)
 
         def transpose_chunk(name):
             words = raw[name][:].bitcast(F32)
+            grouped = {}
+
+            def quantise(r):
+                first = r * PASSES * P
+                nc.vector.quantize_mx(
+                    out=in_codes[name][:, first : first + PASSES * P].bitcast(FP8X4),
+                    scales=in_scales[name][:, first : first + PASSES * P],
+                    in_=grouped[r][:],
+                )
+
             for r in range(TILES):
                 bank = work.tile([P, PASSES, 2, P], F32, tag="work")
                 for c in range(PASSES):
@@ -85,23 +102,23 @@ def tile_attentionnet_pa_kernel(tc, x, wq, wk, out):
                         nc.tensor.transpose(
                             bank[:, c, u, :], words[:, first : first + P], identity[:]
                         )
-                grouped = stage.tile(
-                    [P, PASSES * P * PACK], BF16, tag="grouped_in", align_bytes=64
+                grouped[r] = stage.tile(
+                    [P, PASSES * P * PACK],
+                    BF16,
+                    name="grouped_in",
+                    tag="grouped_in",
+                    align_bytes=64,
                 )
-                dst = grouped[:].bitcast(F32).rearrange(
-                    "p (c r u) -> p c r u", c=PASSES, u=2
+                empty_bank(
+                    r,
+                    grouped[r][:]
+                    .bitcast(F32)
+                    .rearrange("p (c r u) -> p c r u", c=PASSES, u=2),
+                    bank[:].rearrange("p c u r -> p c r u"),
                 )
-                src = bank[:].rearrange("p c u r -> p c r u")
-                if r % 2 == 0:
-                    nc.scalar.copy(out=dst, in_=src)
-                else:
-                    nc.vector.tensor_copy(out=dst, in_=src)
-                first = r * PASSES * P
-                nc.vector.quantize_mx(
-                    out=in_codes[name][:, first : first + PASSES * P].bitcast(FP8X4),
-                    scales=in_scales[name][:, first : first + PASSES * P],
-                    in_=grouped[:],
-                )
+                if r > 0:
+                    quantise(r - 1)
+            quantise(TILES - 1)
 
         qk_codes = {}
         qk_scales = {}
@@ -114,39 +131,57 @@ def tile_attentionnet_pa_kernel(tc, x, wq, wk, out):
                     [P, PASSES * S], U8, name="proj_scales_%s%d" % (name, b), align_bytes=64
                 )
 
-        def project(name, g, b, i):
-            w = "%s%d" % (name, g)
+        def project_pair(name, b, pair, n):
             xb = "x%d" % b
-            bank = work.tile([P, PACK, P], F32, tag="work")
-            for t in range(PACK):
-                for c in range(PASSES):
-                    nc.tensor.matmul_mx(
-                        out=bank[:, t, :],
-                        lhsT=block(in_codes[w], t, c).bitcast(FP8X4),
-                        lhsT_scale=block(in_scales[w], t, c),
-                        rhs=block(in_codes[xb], i, c).bitcast(FP8X4),
-                        rhs_scale=block(in_scales[xb], i, c),
-                        start=(c == 0),
-                        stop=(c == PASSES - 1),
-                    )
-            grouped = stage.tile([P, P * PACK], BF16, tag="grouped_qk", align_bytes=64)
-            nc.scalar.copy(
-                out=grouped[:].rearrange("p (r t) -> p r t", t=PACK),
-                in_=bank[:].rearrange("p t r -> p r t"),
-            )
-            first = g * S + i * P
-            nc.vector.quantize_mx(
-                out=qk_codes[name, b][:, first : first + P].bitcast(FP8X4),
-                scales=qk_scales[name, b][:, first : first + P],
-                in_=grouped[:],
-            )
+            grouped = {}
+            for m, (g, i) in enumerate(pair):
+                w = "%s%d" % (name, g)
+                bank = work.tile([P, PACK, P], F32, tag="work")
+                for t in range(PACK):
+                    for c in range(PASSES):
+                        nc.tensor.matmul_mx(
+                            out=bank[:, t, :],
+                            lhsT=block(in_codes[w], t, c).bitcast(FP8X4),
+                            lhsT_scale=block(in_scales[w], t, c),
+                            rhs=block(in_codes[xb], i, c).bitcast(FP8X4),
+                            rhs_scale=block(in_scales[xb], i, c),
+                            start=(c == 0),
+                            stop=(c == PASSES - 1),
+                        )
+                grouped[m] = stage.tile(
+                    [P, P * PACK], BF16, name="grouped_qk", tag="grouped_qk", align_bytes=64
+                )
+                empty_bank(
+                    n + m,
+                    grouped[m][:].rearrange("p (r t) -> p r t", t=PACK),
+                    bank[:].rearrange("p t r -> p r t"),
+                )
+            for m, (g, i) in enumerate(pair):
+                first = g * S + i * P
+                nc.vector.quantize_mx(
+                    out=qk_codes[name, b][:, first : first + P].bitcast(FP8X4),
+                    scales=qk_scales[name, b][:, first : first + P],
+                    in_=grouped[m][:],
+                )
 
-        def attend(b, i):
-            score = score_pool.tile([P, S], F32, tag="score")
+        def project_keys(g, b):
+            project_pair("k", b, [(g, 0), (g, 1)], 0)
+            project_pair("k", b, [(g, 2), (g, 3)], 2)
+
+        def project_queries(b, i):
+            project_pair("q", b, [(0, i), (1, i)], 2 * (i % 2))
+
+        score = {}
+        shift = {}
+        weights = {}
+        row_sum = {}
+
+        def scores_and_max(b, i):
+            score[b, i] = score_pool.tile([P, S], F32, name="score", tag="score")
             for g in range(PASSES):
                 first = g * S + i * P
                 nc.tensor.matmul_mx(
-                    out=score[:],
+                    out=score[b, i][:],
                     lhsT=qk_codes["q", b][:, first : first + P].bitcast(FP8X4),
                     lhsT_scale=qk_scales["q", b][:, first : first + P],
                     rhs=qk_codes["k", b][:, g * S : (g + 1) * S].bitcast(FP8X4),
@@ -155,46 +190,52 @@ def tile_attentionnet_pa_kernel(tc, x, wq, wk, out):
                     stop=(g == PASSES - 1),
                 )
             row_max = small.tile([P, 1], F32, tag="row_max")
-            nc.vector.reduce_max(out=row_max[:], in_=score[:], axis=mybir.AxisListType.X)
-            shift = small.tile([P, 1], F32, tag="shift")
-            nc.vector.tensor_scalar_mul(out=shift[:], in0=row_max[:], scalar1=-INV_SQRT)
-            weights = stage.tile([P, S], F32, tag="weights")
-            row_sum = small.tile([P, 1], F32, tag="row_sum")
-            nc.scalar.activation(
-                out=weights[:],
-                in_=score[:],
-                func=EXP,
-                bias=shift[:],
-                scale=INV_SQRT,
-                accum_out=row_sum[:],
+            nc.vector.reduce_max(
+                out=row_max[:], in_=score[b, i][:], axis=mybir.AxisListType.X
             )
+            shift[b, i] = small.tile([P, 1], F32, name="shift", tag="shift")
+            nc.vector.tensor_scalar_mul(
+                out=shift[b, i][:], in0=row_max[:], scalar1=-INV_SQRT
+            )
+
+        def exponentials(b, i):
+            weights[b, i] = stage.tile([P, S], F32, name="weights", tag="weights")
+            row_sum[b, i] = small.tile([P, 1], F32, name="row_sum", tag="row_sum")
+            nc.scalar.activation(
+                out=weights[b, i][:],
+                in_=score[b, i][:],
+                func=EXP,
+                bias=shift[b, i][:],
+                scale=INV_SQRT,
+                accum_out=row_sum[b, i][:],
+            )
+
+        def normalise_and_store(b, i):
             inverse = small.tile([P, 1], F32, tag="inverse")
-            nc.vector.reciprocal(out=inverse[:], in_=row_sum[:])
-            nc.vector.tensor_scalar_mul(out=weights[:], in0=weights[:], scalar1=inverse[:])
-            nc.sync.dma_start(out=out[b, i * P : (i + 1) * P, :], in_=weights[:])
-
-        def project_chunk(name, g, b):
-            for i in range(TILES):
-                project(name, g, b, i)
-
-        def project_and_attend(b):
-            for i in range(TILES):
-                project("q", 1, b, i)
-                if i > 0:
-                    attend(b, i - 1)
-            attend(b, TILES - 1)
+            nc.vector.reciprocal(out=inverse[:], in_=row_sum[b, i][:])
+            nc.vector.tensor_scalar_mul(
+                out=weights[b, i][:], in0=weights[b, i][:], scalar1=inverse[:]
+            )
+            nc.sync.dma_start(out=out[b, i * P : (i + 1) * P, :], in_=weights[b, i][:])
 
         transpose_chunk("k0")
         transpose_chunk("x0")
-        project_chunk("k", 0, 0)
+        project_keys(0, 0)
         transpose_chunk("k1")
         transpose_chunk("q0")
-        project_chunk("k", 1, 0)
+        project_keys(1, 0)
         transpose_chunk("q1")
-        project_chunk("q", 0, 0)
         transpose_chunk("x1")
-        project_and_attend(0)
-        project_chunk("k", 0, 1)
-        project_chunk("k", 1, 1)
-        project_chunk("q", 0, 1)
-        project_and_attend(1)
+        tiles = [(b, i) for b in range(B) for i in range(TILES)]
+        for n in range(len(tiles) + 2):
+            if n < len(tiles):
+                b, i = tiles[n]
+                if b > 0 and i == 0:
+                    project_keys(0, b)
+                    project_keys(1, b)
+                project_queries(b, i)
+            if 1 <= n <= len(tiles):
+                scores_and_max(*tiles[n - 1])
+            if n >= 2:
+                exponentials(*tiles[n - 2])
+                normalise_and_store(*tiles[n - 2])

@@ -19,6 +19,7 @@ PASSES = D // K_PASS
 TILES = S // P
 WORDS = D // 2
 INV_SQRT = 1.0 / math.sqrt(D // 8)
+WARM_UP = 6
 
 FLOPS = 2 * (2 * B * S * D * D) + 2 * B * S * S * D
 
@@ -39,6 +40,16 @@ def tile_attentionnet_pa_kernel(tc, x, wq, wk, out):
         one = keep.tile([P, 1], F32, name="one")
         nc.vector.memset(zero[:], 0.0)
         nc.scalar.activation(out=one[:], in_=zero[:], func=EXP)
+
+        zeros = keep.tile([P, S], BF16, name="zeros")
+        nc.vector.memset(zeros[:], 0.0)
+
+        def keep_tensor_engine_busy(count):
+            for n in range(count):
+                unread = work.tile([P, S], F32, tag="work")
+                nc.tensor.matmul(
+                    out=unread[:], lhsT=zeros[:, :P], rhs=zeros[:], start=True, stop=True
+                )
 
         def chunk_of_weights(w, g):
             return w.rearrange("(g p j) k -> g p j k", p=P, j=PACK)[g]
@@ -82,7 +93,7 @@ def tile_attentionnet_pa_kernel(tc, x, wq, wk, out):
             else:
                 nc.scalar.copy(out=dst, in_=src)
 
-        def transpose_chunk(name):
+        def transpose_chunk(name, loads_set_the_pace=False):
             words = raw[name][:].bitcast(F32)
             grouped = {}
 
@@ -102,6 +113,8 @@ def tile_attentionnet_pa_kernel(tc, x, wq, wk, out):
                         nc.tensor.transpose(
                             bank[:, c, u, :], words[:, first : first + P], identity[:]
                         )
+                if loads_set_the_pace:
+                    keep_tensor_engine_busy(1)
                 grouped[r] = stage.tile(
                     [P, PASSES * P * PACK],
                     BF16,
@@ -218,8 +231,9 @@ def tile_attentionnet_pa_kernel(tc, x, wq, wk, out):
             )
             nc.sync.dma_start(out=out[b, i * P : (i + 1) * P, :], in_=weights[b, i][:])
 
-        transpose_chunk("k0")
-        transpose_chunk("x0")
+        keep_tensor_engine_busy(WARM_UP)
+        transpose_chunk("k0", loads_set_the_pace=True)
+        transpose_chunk("x0", loads_set_the_pace=True)
         project_keys(0, 0)
         transpose_chunk("k1")
         transpose_chunk("q0")

from contextlib import ExitStack
import math

import concourse.mybir as mybir
from concourse.masks import make_identity

F32 = mybir.dt.float32
BF16 = mybir.dt.bfloat16
U32 = mybir.dt.uint32
U8 = mybir.dt.uint8
FP8X4 = mybir.dt.float8_e4m3fn_x4
EXP = mybir.ActivationFunctionType.Exp

P = 128
PACK = 4
K_PASS = P * PACK
B, S, D = 2, 512, 1024
PASSES = D // K_PASS
TILES = S // P
WORDS = D // 2
INV_SQRT = 1.0 / math.sqrt(D // 8)
WARM_UP = 6

FLOPS = 2 * (2 * B * S * D * D) + 2 * B * S * S * D


def tile_attentionnet_pa_kernel(tc, x, wq, wk, out):
    nc = tc.nc
    with ExitStack() as ctx:
        keep = ctx.enter_context(tc.tile_pool(name="keep", bufs=1))
        stage = ctx.enter_context(tc.tile_pool(name="stage", bufs=4))
        small = ctx.enter_context(tc.tile_pool(name="small", bufs=4))
        work = ctx.enter_context(tc.psum_pool(name="work", bufs=6))
        score_pool = ctx.enter_context(tc.psum_pool(name="score_pool", bufs=2))
        ctx.enter_context(tc.manual_schedule())

        identity = keep.tile([P, P], F32, name="identity")
        make_identity(nc, identity[:])
        zero = keep.tile([P, 1], F32, name="zero")
        one = keep.tile([P, 1], F32, name="one")
        nc.vector.memset(zero[:], 0.0)
        nc.scalar.activation(out=one[:], in_=zero[:], func=EXP)

        zeros = keep.tile([P, S], BF16, name="zeros")
        nc.vector.memset(zeros[:], 0.0)

        def keep_tensor_engine_busy(count):
            for n in range(count):
                unread = work.tile([P, S], F32, tag="work")
                nc.tensor.matmul(
                    out=unread[:], lhsT=zeros[:, :P], rhs=zeros[:], start=True, stop=True
                )

        def chunk_of_weights(w, g):
            return w.rearrange("(g p j) k -> g p j k", p=P, j=PACK)[g]

        def chunk_of_tokens(b):
            return x[b].rearrange("(i p) k -> p i k", p=P)

        sources = {
            "k0": chunk_of_weights(wk, 0),
            "x0": chunk_of_tokens(0),
            "k1": chunk_of_weights(wk, 1),
            "q0": chunk_of_weights(wq, 0),
            "q1": chunk_of_weights(wq, 1),
            "x1": chunk_of_tokens(1),
        }
        raw = {}
        in_codes = {}
        in_scales = {}
        for name, source in sources.items():
            raw[name] = keep.tile([P, TILES * D], BF16, name="raw_" + name)
            in_codes[name] = keep.tile(
                [P, TILES * PASSES * P], U32, name="codes_" + name, align_bytes=64
            )
            in_scales[name] = keep.tile(
                [P, TILES * PASSES * P], U8, name="scales_" + name, align_bytes=64
            )
            rows = raw[name][:].rearrange("p (r k) -> p r k", r=TILES)
            if name in ("k0", "x0"):
                for r in range(TILES):
                    nc.sync.dma_start(out=rows[:, r, :], in_=source[:, r, :])
            else:
                nc.sync.dma_start(out=rows, in_=source)

        def block(codes_or_scales, r, c):
            first = (r * PASSES + c) * P
            return codes_or_scales[:, first : first + P]

        def empty_bank(n, dst, src):
            if n % 4 == 1:
                nc.vector.tensor_copy(out=dst, in_=src)
            else:
                nc.scalar.copy(out=dst, in_=src)

        def transpose_chunk(name, loads_set_the_pace=False):
            words = raw[name][:].bitcast(F32)
            grouped = {}

            def quantise(r):
                first = r * PASSES * P
                nc.vector.quantize_mx(
                    out=in_codes[name][:, first : first + PASSES * P].bitcast(FP8X4),
                    scales=in_scales[name][:, first : first + PASSES * P],
                    in_=grouped[r][:],
                )

            for r in range(TILES):
                bank = work.tile([P, PASSES, 2, P], F32, tag="work")
                for c in range(PASSES):
                    for u in range(2):
                        first = r * WORDS + (2 * c + u) * P
                        nc.tensor.transpose(
                            bank[:, c, u, :], words[:, first : first + P], identity[:]
                        )
                if loads_set_the_pace:
                    keep_tensor_engine_busy(1)
                grouped[r] = stage.tile(
                    [P, PASSES * P * PACK],
                    BF16,
                    name="grouped_in",
                    tag="grouped_in",
                    align_bytes=64,
                )
                empty_bank(
                    r,
                    grouped[r][:]
                    .bitcast(F32)
                    .rearrange("p (c r u) -> p c r u", c=PASSES, u=2),
                    bank[:].rearrange("p c u r -> p c r u"),
                )
                if r > 0:
                    quantise(r - 1)
            quantise(TILES - 1)

        qk_codes = {}
        qk_scales = {}
        for name in ("q", "k"):
            for b in range(B):
                qk_codes[name, b] = keep.tile(
                    [P, PASSES * S], U32, name="proj_codes_%s%d" % (name, b), align_bytes=64
                )
                qk_scales[name, b] = keep.tile(
                    [P, PASSES * S], U8, name="proj_scales_%s%d" % (name, b), align_bytes=64
                )

        def project_pair(name, b, pair, n):
            xb = "x%d" % b
            grouped = {}
            for m, (g, i) in enumerate(pair):
                w = "%s%d" % (name, g)
                bank = work.tile([P, PACK, P], F32, tag="work")
                for t in range(PACK):
                    for c in range(PASSES):
                        nc.tensor.matmul_mx(
                            out=bank[:, t, :],
                            lhsT=block(in_codes[w], t, c).bitcast(FP8X4),
                            lhsT_scale=block(in_scales[w], t, c),
                            rhs=block(in_codes[xb], i, c).bitcast(FP8X4),
                            rhs_scale=block(in_scales[xb], i, c),
                            start=(c == 0),
                            stop=(c == PASSES - 1),
                        )
                grouped[m] = stage.tile(
                    [P, P * PACK], BF16, name="grouped_qk", tag="grouped_qk", align_bytes=64
                )
                empty_bank(
                    n + m,
                    grouped[m][:].rearrange("p (r t) -> p r t", t=PACK),
                    bank[:].rearrange("p t r -> p r t"),
                )
            for m, (g, i) in enumerate(pair):
                first = g * S + i * P
                nc.vector.quantize_mx(
                    out=qk_codes[name, b][:, first : first + P].bitcast(FP8X4),
                    scales=qk_scales[name, b][:, first : first + P],
                    in_=grouped[m][:],
                )

        def project_keys(g, b):
            project_pair("k", b, [(g, 0), (g, 1)], 0)
            project_pair("k", b, [(g, 2), (g, 3)], 2)

        def project_queries(b, i):
            project_pair("q", b, [(0, i), (1, i)], 2 * (i % 2))

        score = {}
        shift = {}
        weights = {}
        row_sum = {}

        def scores_and_max(b, i):
            score[b, i] = score_pool.tile([P, S], F32, name="score", tag="score")
            for g in range(PASSES):
                first = g * S + i * P
                nc.tensor.matmul_mx(
                    out=score[b, i][:],
                    lhsT=qk_codes["q", b][:, first : first + P].bitcast(FP8X4),
                    lhsT_scale=qk_scales["q", b][:, first : first + P],
                    rhs=qk_codes["k", b][:, g * S : (g + 1) * S].bitcast(FP8X4),
                    rhs_scale=qk_scales["k", b][:, g * S : (g + 1) * S],
                    start=(g == 0),
                    stop=(g == PASSES - 1),
                )
            row_max = small.tile([P, 1], F32, tag="row_max")
            nc.vector.reduce_max(
                out=row_max[:], in_=score[b, i][:], axis=mybir.AxisListType.X
            )
            shift[b, i] = small.tile([P, 1], F32, name="shift", tag="shift")
            nc.vector.tensor_scalar_mul(
                out=shift[b, i][:], in0=row_max[:], scalar1=-INV_SQRT
            )

        def exponentials(b, i):
            weights[b, i] = stage.tile([P, S], F32, name="weights", tag="weights")
            row_sum[b, i] = small.tile([P, 1], F32, name="row_sum", tag="row_sum")
            nc.scalar.activation(
                out=weights[b, i][:],
                in_=score[b, i][:],
                func=EXP,
                bias=shift[b, i][:],
                scale=INV_SQRT,
                accum_out=row_sum[b, i][:],
            )

        def normalise_and_store(b, i):
            inverse = small.tile([P, 1], F32, tag="inverse")
            nc.vector.reciprocal(out=inverse[:], in_=row_sum[b, i][:])
            nc.vector.tensor_scalar_mul(
                out=weights[b, i][:], in0=weights[b, i][:], scalar1=inverse[:]
            )
            nc.sync.dma_start(out=out[b, i * P : (i + 1) * P, :], in_=weights[b, i][:])

        keep_tensor_engine_busy(WARM_UP)
        transpose_chunk("k0", loads_set_the_pace=True)
        transpose_chunk("x0", loads_set_the_pace=True)
        project_keys(0, 0)
        transpose_chunk("k1")
        transpose_chunk("q0")
        project_keys(1, 0)
        transpose_chunk("q1")
        transpose_chunk("x1")
        tiles = [(b, i) for b in range(B) for i in range(TILES)]
        for n in range(len(tiles) + 2):
            if n < len(tiles):
                b, i = tiles[n]
                if b > 0 and i == 0:
                    project_keys(0, b)
                    project_keys(1, b)
                project_queries(b, i)
            if 1 <= n <= len(tiles):
                scores_and_max(*tiles[n - 1])
            if n >= 2:
                exponentials(*tiles[n - 2])
                normalise_and_store(*tiles[n - 2])
